import numpy as np
import ml_dtypes


def mxq(x, axis, fmt="e4m3"):
    dtype, down = {"e4m3": (ml_dtypes.float8_e4m3fn, 7), "e5m2": (ml_dtypes.float8_e5m2, 14)}[fmt]
    v = np.moveaxis(np.asarray(x, np.float32).astype(ml_dtypes.bfloat16).astype(np.float64), axis, -1)
    blocks = v.reshape(v.shape[:-1] + (-1, 32))
    amax = np.abs(blocks).max(-1, keepdims=True)
    byte = np.maximum(np.where(amax > 0, np.frexp(amax)[1] - 1 + 127, 0) - down, 1)
    scale = np.exp2(byte - 127.0)
    codes = (blocks / scale).astype(np.float32).astype(dtype).astype(np.float64)
    return np.moveaxis((codes * scale).reshape(v.shape), -1, axis)


WIDE = False


def mx_kscale(k):
    if not WIDE:
        return np.ones(k)
    levels = np.array([10, -10, 5, -5, 0])
    if k % 512:
        return np.exp2(np.random.permutation(np.resize(levels, k // 32))).repeat(32)
    a = np.empty((k // 512, 16))
    for p in range(k // 512):
        a[p, :8] = np.random.permutation(np.resize(levels, 8))
        for g in range(8):
            far = levels[np.abs(levels - a[p, g]) >= 10]
            a[p, g + 8] = far[np.random.randint(len(far))]
    return np.exp2(a.ravel()).repeat(32)


BF16 = ml_dtypes.bfloat16


def bf(x):
    return np.asarray(x, np.float32).astype(BF16)


def f64(x):
    return np.asarray(x).astype(np.float64)


B, T, E, H, FF = 4, 1024, 1024, 8, 512
EPS = 1e-5


def layernorm(r, g):
    mu = r.mean(-1, keepdims=True)
    var = ((r - mu) ** 2).mean(-1, keepdims=True)
    return (r - mu) / np.sqrt(var + EPS) * g


def setup_inputs():
    t = mx_kscale(FF)
    z = np.random.standard_normal((B, T, FF))
    return {
        "y_act": bf(z * z / (1.0 + np.exp(-z)) * t),
        "h": bf(np.random.standard_normal((B, T, E))),
        "W2": bf(np.random.standard_normal((FF, E)) / np.sqrt(FF) / t[:, None]),
        "b2": bf(np.random.standard_normal(E) * 0.1),
        "g2": bf(1.0 + np.random.standard_normal(E) * 0.1),
    }


def core(y_act, h, W2, b2, g2):
    ff = (mxq(f64(y_act), 2, "e4m3") @ mxq(f64(W2), 0, "e4m3")) + f64(b2)
    return layernorm(ff + f64(h), f64(g2))


def e4m3fn_bytes(y):
    return np.clip(np.asarray(y, np.float64), -448.0, 448.0).astype(np.float32).astype(ml_dtypes.float8_e4m3fn).view(np.uint8)


Y_SCALE = 220.0


def reference(y_act, h, W2, b2, g2):
    out = core(y_act, h, W2, b2, g2)
    return out, e4m3fn_bytes(out * Y_SCALE)

@@ -1,0 +1,310 @@
+from contextlib import ExitStack
+
+import concourse.mybir as mybir
+from concourse.masks import make_identity
+
+F32 = mybir.dt.float32
+BF16 = mybir.dt.bfloat16
+U32 = mybir.dt.uint32
+U8 = mybir.dt.uint8
+FP8X4 = mybir.dt.float8_e4m3fn_x4
+FP8 = mybir.dt.float8_e4m3fn
+ALU = mybir.AluOpType
+ACT = mybir.ActivationFunctionType
+
+TOKENS, K, E = 4096, 512, 1024
+EPS = 1e-5
+Y_SCALE = 220.0
+FLOPS = 2 * TOKENS * K * E
+
+P = 128
+J = 4
+GROUP = P * J
+NG = TOKENS // GROUP
+NT = NG * J
+BANK = 512
+
+LA = 3
+LR = 2
+SC_ENGINE = ("S", "G", "S", "G")
+E0_ENGINE = ("V", "V")
+
+
+def tile_transformerblock_pb_t_kernel(tc, y_act, h, W2, b2, g2, out_0, out_1):
+    nc = tc.nc
+    yf = y_act.flatten_outer_dims()
+    hf = h.flatten_outer_dims()
+    o0f = out_0.flatten_outer_dims()
+    o1f = out_1.flatten_outer_dims()
+
+    with ExitStack() as ctx:
+        const = ctx.enter_context(tc.tile_pool(name="const", bufs=1))
+        ypool = ctx.enter_context(tc.tile_pool(name="ypool", bufs=4))
+        hpool = ctx.enter_context(tc.tile_pool(name="hpool", bufs=4))
+        qpool = ctx.enter_context(tc.tile_pool(name="qpool", bufs=2))
+        hbpool = ctx.enter_context(tc.tile_pool(name="hbpool", bufs=LA + 2))
+        rpool = ctx.enter_context(tc.tile_pool(name="rpool", bufs=3))
+        tpool = ctx.enter_context(tc.tile_pool(name="tpool", bufs=LR + 2))
+        opool = ctx.enter_context(tc.tile_pool(name="opool", bufs=5))
+        bpool = ctx.enter_context(tc.tile_pool(name="bpool", bufs=2))
+        stat = ctx.enter_context(tc.tile_pool(name="stat", bufs=6))
+        ps_t = ctx.enter_context(tc.psum_pool(name="ps_t", bufs=2))
+        ps_m = ctx.enter_context(tc.psum_pool(name="ps_m", bufs=4))
+        ps_g = ctx.enter_context(tc.psum_pool(name="ps_g", bufs=1))
+        ctx.enter_context(tc.manual_schedule())
+
+        ident = const.tile([P, P], F32, name="ident")
+        ones = const.tile([P, P], BF16, name="ones")
+        cst = const.tile([P, 2 * E], BF16, name="cst")
+        b2_bc = const.tile([P, E], BF16, name="b2_bc")
+        eps_t = const.tile([P, 1], F32, name="eps_t")
+        warm = const.tile([P, 1], F32, name="warm")
+        junk = const.tile([P, E], BF16, name="junk")
+        w_codes = const.tile([P, E], U32, name="w_codes", align_bytes=64)
+        w_scales = const.tile([P, E], U8, name="w_scales", align_bytes=64)
+        w_raw = [const.tile([P, J, BANK], BF16, name="w_raw%d" % c) for c in range(2)]
+        w_grp = [const.tile([P, J * BANK], BF16, name="w_grp%d" % c, align_bytes=64) for c in range(2)]
+        h_first = [const.tile([P, E], BF16, name="h_first%d" % j) for j in range(J)]
+        g2_ps = [ps_g.tile([P, BANK], F32, name="g2_ps%d" % c) for c in range(2)]
+
+        y_sb, h_sb, xt, grp, codes, scales, o8 = {}, {}, {}, {}, {}, {}, {}
+        hb, mm, r, rsum, negmu, ssq, std, rstd, t, o0t = {}, {}, {}, {}, {}, {}, {}, {}, {}, {}
+
+        def rows(ap, g):
+            return ap[g * GROUP : (g + 1) * GROUP, :]
+
+        def load_y(g):
+            y_sb[g] = ypool.tile([P, J, K], BF16, name="y_sb")
+            nc.sync.dma_start(out=y_sb[g][:], in_=rows(yf, g).rearrange("(p j) k -> p j k", j=J))
+
+        def load_h(g):
+            h_sb[g] = hpool.tile([P, J, E], BF16, name="h_sb")
+            nc.sync.dma_start(out=h_sb[g][:], in_=rows(hf, g).rearrange("(p j) n -> p j n", j=J))
+
+        def load_h_first(j):
+            nc.sync.dma_start(out=h_first[j][:], in_=rows(hf, 0).rearrange("(p j) n -> p j n", j=J)[:, j, :])
+
+        def load_w(c):
+            nc.sync.dma_start(
+                out=w_raw[c][:], in_=W2[:, c * BANK : (c + 1) * BANK].rearrange("(p j) n -> p j n", j=J)
+            )
+
+        def transposes(g):
+            xt[g] = []
+            for b in range(2):
+                bank = ps_t.tile([P, 2, 2, P], F32, name="xt")
+                xt[g].append(bank)
+                for a in range(2):
+                    words = y_sb[g][:, 2 * b + a, :].bitcast(F32)
+                    for u in range(2):
+                        nc.tensor.transpose(bank[:, a, u, :], words[:, u : K // 2 : 2], ident[:])
+
+        def empty_transposes(g, b):
+            if b == 0:
+                grp[g] = qpool.tile([P, 4 * GROUP], BF16, name="grp", align_bytes=64)
+            dst = grp[g][:].bitcast(F32)[:, b * BANK : (b + 1) * BANK].rearrange("q (a t u) -> q a t u", a=2, u=2)
+            src = xt[g][b][:].rearrange("q a u t -> q a t u")
+            if E0_ENGINE[b] == "V":
+                nc.vector.tensor_copy(out=dst, in_=src)
+            else:
+                nc.scalar.copy(out=dst, in_=src)
+
+        def quantize_y(g):
+            codes[g] = qpool.tile([P, GROUP], U32, name="codes", align_bytes=64)
+            scales[g] = qpool.tile([P, GROUP], U8, name="scales", align_bytes=64)
+            nc.vector.quantize_mx(out=codes[g][:].bitcast(FP8X4), scales=scales[g][:], in_=grp[g][:])
+
+        def interleave_w(c, engine):
+            dst = w_grp[c][:].rearrange("p (n j) -> p n j", j=J)
+            src = w_raw[c][:].rearrange("p j n -> p n j")
+            if engine == "V":
+                nc.vector.tensor_copy(out=dst, in_=src)
+            else:
+                nc.scalar.copy(out=dst, in_=src)
+
+        def quantize_w(c):
+            cols = slice(c * BANK, (c + 1) * BANK)
+            nc.vector.quantize_mx(out=w_codes[:, cols].bitcast(FP8X4), scales=w_scales[:, cols], in_=w_grp[c][:])
+
+        def add_bias(i):
+            g, j = divmod(i, J)
+            hb[i] = hbpool.tile([P, E], F32, name="hb")
+            src = h_first[j][:] if g == 0 else h_sb[g][:, j, :]
+            nc.gpsimd.tensor_tensor(out=hb[i][:], in0=src, in1=b2_bc[:], op=ALU.add)
+
+        def matmuls(i):
+            g, j = divmod(i, J)
+            toks = slice(j * P, (j + 1) * P)
+            mm[i] = []
+            for c in range(2):
+                cols = slice(c * BANK, (c + 1) * BANK)
+                acc = ps_m.tile([P, BANK], F32, name="acc")
+                mm[i].append(acc)
+                nc.tensor.matmul_mx(
+                    out=acc[:],
+                    lhsT=codes[g][:, toks].bitcast(FP8X4),
+                    lhsT_scale=scales[g][:, toks],
+                    rhs=w_codes[:, cols].bitcast(FP8X4),
+                    rhs_scale=w_scales[:, cols],
+                    start=True,
+                    stop=True,
+                )
+
+        def residual(i):
+            r[i] = rpool.tile([P, E], F32, name="r")
+            rsum[i] = stat.tile([P, 2], F32, name="rsum")
+            for c in range(2):
+                cols = slice(c * BANK, (c + 1) * BANK)
+                nc.vector.scalar_tensor_tensor(
+                    out=r[i][:, cols],
+                    in0=mm[i][c][:],
+                    scalar=1.0,
+                    in1=hb[i][:, cols],
+                    op0=ALU.mult,
+                    op1=ALU.add,
+                    accum_out=rsum[i][:, c : c + 1],
+                )
+
+        def mean(i):
+            negmu[i] = stat.tile([P, 1], F32, name="negmu")
+            part = stat.tile([P, 2], F32, name="part")
+            nc.vector.tensor_scalar(
+                out=part[:],
+                in0=rsum[i][:],
+                scalar1=-1.0 / E,
+                scalar2=None,
+                op0=ALU.mult,
+                op1=ALU.add,
+                accum_out=negmu[i][:],
+            )
+
+        def squares(i):
+            ssq[i] = stat.tile([P, 1], F32, name="ssq")
+            nc.scalar.activation(
+                out=junk[:], in_=r[i][:], func=ACT.Square, bias=negmu[i][:, 0:1], scale=1.0, accum_out=ssq[i][:]
+            )
+
+        def root(i):
+            std[i] = stat.tile([P, 1], F32, name="std")
+            nc.scalar.activation(out=std[i][:], in_=ssq[i][:], func=ACT.Sqrt, bias=eps_t[:, 0:1], scale=1.0 / E)
+
+        def recip(i):
+            rstd[i] = stat.tile([P, 1], F32, name="rstd")
+            nc.vector.reciprocal(out=rstd[i][:], in_=std[i][:])
+
+        def gain(i):
+            t[i] = tpool.tile([P, E], F32, name="t")
+            for c in range(2):
+                cols = slice(c * BANK, (c + 1) * BANK)
+                nc.vector.scalar_tensor_tensor(
+                    out=t[i][:, cols],
+                    in0=r[i][:, cols],
+                    scalar=negmu[i][:, 0:1],
+                    in1=g2_ps[c][:],
+                    op0=ALU.add,
+                    op1=ALU.mult,
+                )
+
+        def scale_by_rstd(i):
+            o0t[i] = opool.tile([P, E], F32, name="o0t")
+            if SC_ENGINE[i % J] == "S":
+                nc.scalar.activation(out=o0t[i][:], in_=t[i][:], func=ACT.Copy, scale=rstd[i][:, 0:1])
+            else:
+                nc.gpsimd.tensor_scalar(
+                    out=o0t[i][:], in0=t[i][:], scalar1=rstd[i][:, 0:1], scalar2=1.0, op0=ALU.mult, op1=ALU.mult
+                )
+
+        def cast(i):
+            g, j = divmod(i, J)
+            if j == 0:
+                o8[g] = bpool.tile([P, J * E], FP8, name="o8")
+            nc.scalar.activation(
+                out=o8[g][:, j * E : (j + 1) * E], in_=o0t[i][:], func=ACT.Copy, scale=Y_SCALE, saturate=False
+            )
+
+        def store_f32(i):
+            g, j = divmod(i, J)
+            nc.sync.dma_start(out=rows(o0f, g).rearrange("(p j) n -> p j n", j=J)[:, j, :], in_=o0t[i][:])
+
+        def store_bytes(g):
+            nc.sync.dma_start(out=rows(o1f, g).rearrange("(p j) n -> p (j n)", j=J), in_=o8[g][:].bitcast(U8))
+
+        nc.vector.memset(cst[:], 0.0)
+        nc.vector.memset(ones[:], 1.0)
+        nc.vector.memset(eps_t[:], EPS)
+        make_identity(nc, ident[:])
+        nc.scalar.dma_start(out=cst[0:1, 0:E], in_=b2.unsqueeze(0))
+        nc.scalar.dma_start(out=cst[0:1, E : 2 * E], in_=g2.unsqueeze(0))
+        load_y(0)
+        load_h_first(0)
+        load_w(0)
+        load_w(1)
+        for j in range(1, J):
+            load_h_first(j)
+        for g in range(1, 4):
+            load_y(g)
+            load_h(g)
+        load_h(4)
+        nc.scalar.activation(out=warm[:], in_=eps_t[:], func=ACT.Sqrt)
+
+        transposes(0)
+        b2_ps = []
+        for c in range(2):
+            acc = ps_m.tile([P, BANK], F32, name="acc")
+            b2_ps.append(acc)
+            nc.tensor.matmul(acc[:], lhsT=ones[:], rhs=cst[:, c * BANK : (c + 1) * BANK], start=True, stop=True)
+        for c in range(2):
+            nc.tensor.matmul(
+                g2_ps[c][:], lhsT=ones[:], rhs=cst[:, E + c * BANK : E + (c + 1) * BANK], start=True, stop=True
+            )
+        for c in range(2):
+            nc.scalar.copy(out=b2_bc[:, c * BANK : (c + 1) * BANK], in_=b2_ps[c][:])
+        empty_transposes(0, 0)
+        empty_transposes(0, 1)
+        quantize_y(0)
+        interleave_w(0, "V")
+        interleave_w(1, "S")
+        quantize_w(0)
+        quantize_w(1)
+        for i in range(LA):
+            add_bias(i)
+        matmuls(0)
+        transposes(1)
+
+        for s in range(NT + LR + 1):
+            g, j = divmod(s, J)
+            if s + LA < NT:
+                add_bias(s + LA)
+            if s + 1 < NT:
+                matmuls(s + 1)
+            if j == 3 and g + 2 < NG:
+                transposes(g + 2)
+            if s < NT:
+                residual(s)
+            if 0 <= s - 1 < NT:
+                gain(s - 1)
+            if s < NT:
+                mean(s)
+            if 0 <= s - LR < NT:
+                recip(s - LR)
+            if g + 1 < NG:
+                if j < 2:
+                    empty_transposes(g + 1, j)
+                elif j == 2:
+                    quantize_y(g + 1)
+            if s < NT:
+                squares(s)
+            if 0 <= s - LR - 1 < NT:
+                cast(s - LR - 1)
+            if s < NT:
+                root(s)
+            if 0 <= s - LR < NT:
+                scale_by_rstd(s - LR)
+            if j == 1 and g + 4 < NG:
+                load_y(g + 4)
+                if g > 0:
+                    load_h(g + 4)
+            if 0 <= s - LR < NT:
+                store_f32(s - LR)
+            if 0 <= s - LR - 1 < NT and (s - LR - 1) % J == J - 1:
+                store_bytes((s - LR - 1) // J)

@@ -26,8 +26,27 @@ BANK = 512
 
 LA = 3
 LR = 2
-SC_ENGINE = ("S", "G", "S", "G")
-E0_ENGINE = ("V", "V")
+
+
+def scaler(i):
+    g, j = divmod(i, J)
+    if i >= NT - 2:
+        return "V"
+    if i >= NT - 6:
+        return "G"
+    if g > 0 and (j == 0 or (j == 2 and g % 2 == 1)):
+        return "G"
+    return "S"
+
+
+def emptier(g, b):
+    if g == 0:
+        return "VS"[b]
+    return "S" if (b == 0 and g >= 2) else "V"
+
+
+def caster(i):
+    return "V" if i == NT - 1 else "S"
 
 
 def tile_transformerblock_pb_t_kernel(tc, y_act, h, W2, b2, g2, out_0, out_1):
@@ -47,6 +66,7 @@ def tile_transformerblock_pb_t_kernel(tc, y_act, h, W2, b2, g2, out_0, out_1):
         tpool = ctx.enter_context(tc.tile_pool(name="tpool", bufs=LR + 2))
         opool = ctx.enter_context(tc.tile_pool(name="opool", bufs=5))
         bpool = ctx.enter_context(tc.tile_pool(name="bpool", bufs=2))
+        upool = ctx.enter_context(tc.tile_pool(name="upool", bufs=1))
         stat = ctx.enter_context(tc.tile_pool(name="stat", bufs=6))
         ps_t = ctx.enter_context(tc.psum_pool(name="ps_t", bufs=2))
         ps_m = ctx.enter_context(tc.psum_pool(name="ps_m", bufs=4))
@@ -104,7 +124,7 @@ def tile_transformerblock_pb_t_kernel(tc, y_act, h, W2, b2, g2, out_0, out_1):
                 grp[g] = qpool.tile([P, 4 * GROUP], BF16, name="grp", align_bytes=64)
             dst = grp[g][:].bitcast(F32)[:, b * BANK : (b + 1) * BANK].rearrange("q (a t u) -> q a t u", a=2, u=2)
             src = xt[g][b][:].rearrange("q a u t -> q a t u")
-            if E0_ENGINE[b] == "V":
+            if emptier(g, b) == "V":
                 nc.vector.tensor_copy(out=dst, in_=src)
             else:
                 nc.scalar.copy(out=dst, in_=src)
@@ -114,9 +134,10 @@ def tile_transformerblock_pb_t_kernel(tc, y_act, h, W2, b2, g2, out_0, out_1):
             scales[g] = qpool.tile([P, GROUP], U8, name="scales", align_bytes=64)
             nc.vector.quantize_mx(out=codes[g][:].bitcast(FP8X4), scales=scales[g][:], in_=grp[g][:])
 
-        def interleave_w(c, engine):
-            dst = w_grp[c][:].rearrange("p (n j) -> p n j", j=J)
-            src = w_raw[c][:].rearrange("p j n -> p n j")
+        def interleave_w(c, half, engine):
+            cols = slice(half * BANK // 2, (half + 1) * BANK // 2)
+            dst = w_grp[c][:].rearrange("p (n j) -> p n j", j=J)[:, cols, :]
+            src = w_raw[c][:, :, cols].rearrange("p j n -> p n j")
             if engine == "V":
                 nc.vector.tensor_copy(out=dst, in_=src)
             else:
@@ -130,7 +151,12 @@ def tile_transformerblock_pb_t_kernel(tc, y_act, h, W2, b2, g2, out_0, out_1):
             g, j = divmod(i, J)
             hb[i] = hbpool.tile([P, E], F32, name="hb")
             src = h_first[j][:] if g == 0 else h_sb[g][:, j, :]
-            nc.gpsimd.tensor_tensor(out=hb[i][:], in0=src, in1=b2_bc[:], op=ALU.add)
+            if i == 0:
+                for c in range(2):
+                    cols = slice(c * BANK, (c + 1) * BANK)
+                    nc.vector.tensor_tensor(out=hb[i][:, cols], in0=src[:, cols], in1=b2_ps[c][:], op=ALU.add)
+            else:
+                nc.gpsimd.tensor_tensor(out=hb[i][:], in0=src, in1=b2_bc[:], op=ALU.add)
 
         def matmuls(i):
             g, j = divmod(i, J)
@@ -207,8 +233,10 @@ def tile_transformerblock_pb_t_kernel(tc, y_act, h, W2, b2, g2, out_0, out_1):
 
         def scale_by_rstd(i):
             o0t[i] = opool.tile([P, E], F32, name="o0t")
-            if SC_ENGINE[i % J] == "S":
+            if scaler(i) == "S":
                 nc.scalar.activation(out=o0t[i][:], in_=t[i][:], func=ACT.Copy, scale=rstd[i][:, 0:1])
+            elif scaler(i) == "V":
+                nc.vector.tensor_scalar(out=o0t[i][:], in0=t[i][:], scalar1=rstd[i][:, 0:1], scalar2=None, op0=ALU.mult)
             else:
                 nc.gpsimd.tensor_scalar(
                     out=o0t[i][:], in0=t[i][:], scalar1=rstd[i][:, 0:1], scalar2=1.0, op0=ALU.mult, op1=ALU.mult
@@ -218,9 +246,14 @@ def tile_transformerblock_pb_t_kernel(tc, y_act, h, W2, b2, g2, out_0, out_1):
             g, j = divmod(i, J)
             if j == 0:
                 o8[g] = bpool.tile([P, J * E], FP8, name="o8")
-            nc.scalar.activation(
-                out=o8[g][:, j * E : (j + 1) * E], in_=o0t[i][:], func=ACT.Copy, scale=Y_SCALE, saturate=False
-            )
+            if caster(i) == "S":
+                nc.scalar.activation(
+                    out=o8[g][:, j * E : (j + 1) * E], in_=o0t[i][:], func=ACT.Copy, scale=Y_SCALE, saturate=False
+                )
+            else:
+                u = upool.tile([P, E], F32, name="u")
+                nc.vector.tensor_scalar(out=u[:], in0=o0t[i][:], scalar1=Y_SCALE, scalar2=None, op0=ALU.mult)
+                nc.vector.tensor_copy(out=o8[g][:, j * E : (j + 1) * E], in_=u[:], saturate=False)
 
         def store_f32(i):
             g, j = divmod(i, J)
@@ -229,15 +262,22 @@ def tile_transformerblock_pb_t_kernel(tc, y_act, h, W2, b2, g2, out_0, out_1):
         def store_bytes(g):
             nc.sync.dma_start(out=rows(o1f, g).rearrange("(p j) n -> p (j n)", j=J), in_=o8[g][:].bitcast(U8))
 
+        def store_bytes_of_tile(i):
+            g, j = divmod(i, J)
+            nc.sync.dma_start(
+                out=rows(o1f, g).rearrange("(p j) n -> p j n", j=J)[:, j, :],
+                in_=o8[g][:, j * E : (j + 1) * E].bitcast(U8),
+            )
+
         nc.vector.memset(cst[:], 0.0)
         nc.vector.memset(ones[:], 1.0)
         nc.vector.memset(eps_t[:], EPS)
         make_identity(nc, ident[:])
         nc.scalar.dma_start(out=cst[0:1, 0:E], in_=b2.unsqueeze(0))
         nc.scalar.dma_start(out=cst[0:1, E : 2 * E], in_=g2.unsqueeze(0))
-        load_y(0)
-        load_h_first(0)
         load_w(0)
+        load_h_first(0)
+        load_y(0)
         load_w(1)
         for j in range(1, J):
             load_h_first(j)
@@ -247,7 +287,6 @@ def tile_transformerblock_pb_t_kernel(tc, y_act, h, W2, b2, g2, out_0, out_1):
         load_h(4)
         nc.scalar.activation(out=warm[:], in_=eps_t[:], func=ACT.Sqrt)
 
-        transposes(0)
         b2_ps = []
         for c in range(2):
             acc = ps_m.tile([P, BANK], F32, name="acc")
@@ -257,54 +296,67 @@ def tile_transformerblock_pb_t_kernel(tc, y_act, h, W2, b2, g2, out_0, out_1):
             nc.tensor.matmul(
                 g2_ps[c][:], lhsT=ones[:], rhs=cst[:, E + c * BANK : E + (c + 1) * BANK], start=True, stop=True
             )
-        for c in range(2):
-            nc.scalar.copy(out=b2_bc[:, c * BANK : (c + 1) * BANK], in_=b2_ps[c][:])
+        interleave_w(0, 0, "V")
+        interleave_w(0, 1, "S")
+        add_bias(0)
+        transposes(0)
         empty_transposes(0, 0)
         empty_transposes(0, 1)
-        quantize_y(0)
-        interleave_w(0, "V")
-        interleave_w(1, "S")
         quantize_w(0)
+        quantize_y(0)
+        interleave_w(1, 0, "V")
+        interleave_w(1, 1, "S")
         quantize_w(1)
-        for i in range(LA):
-            add_bias(i)
+        for c in range(2):
+            nc.scalar.copy(out=b2_bc[:, c * BANK : (c + 1) * BANK], in_=b2_ps[c][:])
         matmuls(0)
-        transposes(1)
+        for i in range(1, LA):
+            add_bias(i)
 
         for s in range(NT + LR + 1):
             g, j = divmod(s, J)
+            si = s - LR
+            fi = s - LR - 1
             if s + LA < NT:
                 add_bias(s + LA)
+            if j == 3 and g + 1 < NG:
+                quantize_y(g + 1)
             if s + 1 < NT:
                 matmuls(s + 1)
-            if j == 3 and g + 2 < NG:
-                transposes(g + 2)
+            if j == 0 and g + 1 < NG:
+                transposes(g + 1)
             if s < NT:
                 residual(s)
+            if s == NT - 1:
+                mean(s)
             if 0 <= s - 1 < NT:
                 gain(s - 1)
-            if s < NT:
+            if s < NT - 1:
                 mean(s)
-            if 0 <= s - LR < NT:
-                recip(s - LR)
-            if g + 1 < NG:
-                if j < 2:
-                    empty_transposes(g + 1, j)
-                elif j == 2:
-                    quantize_y(g + 1)
+            if 0 <= si < NT:
+                recip(si)
+            if g + 1 < NG and j in (1, 2):
+                empty_transposes(g + 1, j - 1)
+            if 0 <= si < NT and scaler(si) == "V":
+                scale_by_rstd(si)
+            if 0 <= fi < NT and caster(fi) == "V":
+                cast(fi)
             if s < NT:
                 squares(s)
-            if 0 <= s - LR - 1 < NT:
-                cast(s - LR - 1)
+            if 0 <= fi < NT and caster(fi) == "S":
+                cast(fi)
             if s < NT:
                 root(s)
-            if 0 <= s - LR < NT:
-                scale_by_rstd(s - LR)
+            if 0 <= si < NT and scaler(si) != "V":
+                scale_by_rstd(si)
             if j == 1 and g + 4 < NG:
                 load_y(g + 4)
                 if g > 0:
                     load_h(g + 4)
-            if 0 <= s - LR < NT:
-                store_f32(s - LR)
-            if 0 <= s - LR - 1 < NT and (s - LR - 1) % J == J - 1:
-                store_bytes((s - LR - 1) // J)
+            if 0 <= si < NT:
+                store_f32(si)
+            if 0 <= fi < NT:
+                if fi >= NT - J:
+                    store_bytes_of_tile(fi)
+                elif fi % J == J - 1:
+                    store_bytes(fi // J)

@@ -30,23 +30,21 @@ LR = 2
 
 def scaler(i):
     g, j = divmod(i, J)
-    if i >= NT - 2:
+    if i >= NT - 3:
         return "V"
-    if i >= NT - 6:
+    if i >= NT - 8:
         return "G"
-    if g > 0 and (j == 0 or (j == 2 and g % 2 == 1)):
-        return "G"
-    return "S"
+    return "G" if j % 2 == 0 else "S"
 
 
 def emptier(g, b):
     if g == 0:
         return "VS"[b]
-    return "S" if (b == 0 and g >= 2) else "V"
+    return "S" if b == 0 else "V"
 
 
 def caster(i):
-    return "V" if i == NT - 1 else "S"
+    return "V" if i == NT - 2 else "S"
 
 
 def tile_transformerblock_pb_t_kernel(tc, y_act, h, W2, b2, g2, out_0, out_1):

@@ -30,21 +30,21 @@ LR = 2
 
 def scaler(i):
     g, j = divmod(i, J)
-    if i >= NT - 3:
+    if i >= NT - 4:
         return "V"
-    if i >= NT - 8:
+    if i >= NT - 6:
         return "G"
-    return "G" if j % 2 == 0 else "S"
+    return "G" if (g > 0 and j == 0) else "S"
 
 
 def emptier(g, b):
     if g == 0:
         return "VS"[b]
-    return "S" if b == 0 else "V"
+    return "S" if (b == 0 and g >= 2 and g % 2 == 0) else "V"
 
 
 def caster(i):
-    return "V" if i == NT - 2 else "S"
+    return "V" if i == NT - 1 else "S"
 
 
 def tile_transformerblock_pb_t_kernel(tc, y_act, h, W2, b2, g2, out_0, out_1):
@@ -237,7 +237,7 @@ def tile_transformerblock_pb_t_kernel(tc, y_act, h, W2, b2, g2, out_0, out_1):
                 nc.vector.tensor_scalar(out=o0t[i][:], in0=t[i][:], scalar1=rstd[i][:, 0:1], scalar2=None, op0=ALU.mult)
             else:
                 nc.gpsimd.tensor_scalar(
-                    out=o0t[i][:], in0=t[i][:], scalar1=rstd[i][:, 0:1], scalar2=1.0, op0=ALU.mult, op1=ALU.mult
+                    out=o0t[i][:], in0=t[i][:], scalar1=rstd[i][:, 0:1], scalar2=0.0, op0=ALU.mult, op1=ALU.add
                 )
 
         def cast(i):

@@ -38,13 +38,7 @@ def scaler(i):
 
 
 def emptier(g, b):
-    if g == 0:
-        return "VS"[b]
-    return "S" if (b == 0 and g >= 2 and g % 2 == 0) else "V"
-
-
-def caster(i):
-    return "V" if i == NT - 1 else "S"
+    return "S" if (g == 0 and b == 1) else "V"
 
 
 def tile_transformerblock_pb_t_kernel(tc, y_act, h, W2, b2, g2, out_0, out_1):
@@ -64,7 +58,6 @@ def tile_transformerblock_pb_t_kernel(tc, y_act, h, W2, b2, g2, out_0, out_1):
         tpool = ctx.enter_context(tc.tile_pool(name="tpool", bufs=LR + 2))
         opool = ctx.enter_context(tc.tile_pool(name="opool", bufs=5))
         bpool = ctx.enter_context(tc.tile_pool(name="bpool", bufs=2))
-        upool = ctx.enter_context(tc.tile_pool(name="upool", bufs=1))
         stat = ctx.enter_context(tc.tile_pool(name="stat", bufs=6))
         ps_t = ctx.enter_context(tc.psum_pool(name="ps_t", bufs=2))
         ps_m = ctx.enter_context(tc.psum_pool(name="ps_m", bufs=4))
@@ -244,14 +237,9 @@ def tile_transformerblock_pb_t_kernel(tc, y_act, h, W2, b2, g2, out_0, out_1):
             g, j = divmod(i, J)
             if j == 0:
                 o8[g] = bpool.tile([P, J * E], FP8, name="o8")
-            if caster(i) == "S":
-                nc.scalar.activation(
-                    out=o8[g][:, j * E : (j + 1) * E], in_=o0t[i][:], func=ACT.Copy, scale=Y_SCALE, saturate=False
-                )
-            else:
-                u = upool.tile([P, E], F32, name="u")
-                nc.vector.tensor_scalar(out=u[:], in0=o0t[i][:], scalar1=Y_SCALE, scalar2=None, op0=ALU.mult)
-                nc.vector.tensor_copy(out=o8[g][:, j * E : (j + 1) * E], in_=u[:], saturate=False)
+            nc.scalar.activation(
+                out=o8[g][:, j * E : (j + 1) * E], in_=o0t[i][:], func=ACT.Copy, scale=Y_SCALE, saturate=False
+            )
 
         def store_f32(i):
             g, j = divmod(i, J)
@@ -298,16 +286,17 @@ def tile_transformerblock_pb_t_kernel(tc, y_act, h, W2, b2, g2, out_0, out_1):
         interleave_w(0, 1, "S")
         add_bias(0)
         transposes(0)
-        empty_transposes(0, 0)
-        empty_transposes(0, 1)
         quantize_w(0)
-        quantize_y(0)
         interleave_w(1, 0, "V")
         interleave_w(1, 1, "S")
+        empty_transposes(0, 0)
+        empty_transposes(0, 1)
         quantize_w(1)
+        quantize_y(0)
         for c in range(2):
             nc.scalar.copy(out=b2_bc[:, c * BANK : (c + 1) * BANK], in_=b2_ps[c][:])
         matmuls(0)
+        transposes(1)
         for i in range(1, LA):
             add_bias(i)
 
@@ -317,12 +306,10 @@ def tile_transformerblock_pb_t_kernel(tc, y_act, h, W2, b2, g2, out_0, out_1):
             fi = s - LR - 1
             if s + LA < NT:
                 add_bias(s + LA)
-            if j == 3 and g + 1 < NG:
-                quantize_y(g + 1)
             if s + 1 < NT:
                 matmuls(s + 1)
-            if j == 0 and g + 1 < NG:
-                transposes(g + 1)
+            if j == 3 and g + 2 < NG:
+                transposes(g + 2)
             if s < NT:
                 residual(s)
             if s == NT - 1:
@@ -331,17 +318,17 @@ def tile_transformerblock_pb_t_kernel(tc, y_act, h, W2, b2, g2, out_0, out_1):
                 gain(s - 1)
             if s < NT - 1:
                 mean(s)
+            if j == 2 and g + 1 < NG:
+                quantize_y(g + 1)
             if 0 <= si < NT:
                 recip(si)
-            if g + 1 < NG and j in (1, 2):
-                empty_transposes(g + 1, j - 1)
+            if g + 1 < NG and j in (0, 1):
+                empty_transposes(g + 1, j)
             if 0 <= si < NT and scaler(si) == "V":
                 scale_by_rstd(si)
-            if 0 <= fi < NT and caster(fi) == "V":
-                cast(fi)
             if s < NT:
                 squares(s)
-            if 0 <= fi < NT and caster(fi) == "S":
+            if 0 <= fi < NT:
                 cast(fi)
             if s < NT:
                 root(s)

from contextlib import ExitStack

import concourse.mybir as mybir
from concourse.masks import make_identity

F32 = mybir.dt.float32
BF16 = mybir.dt.bfloat16
U32 = mybir.dt.uint32
U8 = mybir.dt.uint8
FP8X4 = mybir.dt.float8_e4m3fn_x4
FP8 = mybir.dt.float8_e4m3fn
ALU = mybir.AluOpType
ACT = mybir.ActivationFunctionType

TOKENS, K, E = 4096, 512, 1024
EPS = 1e-5
Y_SCALE = 220.0
FLOPS = 2 * TOKENS * K * E

P = 128
J = 4
GROUP = P * J
NG = TOKENS // GROUP
NT = NG * J
BANK = 512

LA = 3
LR = 2


def scaler(i):
    g, j = divmod(i, J)
    if i >= NT - 4:
        return "V"
    if i >= NT - 6:
        return "G"
    return "G" if (g > 0 and j == 0) else "S"


def emptier(g, b):
    return "S" if (g == 0 and b == 1) else "V"


def tile_transformerblock_pb_t_kernel(tc, y_act, h, W2, b2, g2, out_0, out_1):
    nc = tc.nc
    yf = y_act.flatten_outer_dims()
    hf = h.flatten_outer_dims()
    o0f = out_0.flatten_outer_dims()
    o1f = out_1.flatten_outer_dims()

    with ExitStack() as ctx:
        const = ctx.enter_context(tc.tile_pool(name="const", bufs=1))
        ypool = ctx.enter_context(tc.tile_pool(name="ypool", bufs=4))
        hpool = ctx.enter_context(tc.tile_pool(name="hpool", bufs=4))
        qpool = ctx.enter_context(tc.tile_pool(name="qpool", bufs=2))
        hbpool = ctx.enter_context(tc.tile_pool(name="hbpool", bufs=LA + 2))
        rpool = ctx.enter_context(tc.tile_pool(name="rpool", bufs=3))
        tpool = ctx.enter_context(tc.tile_pool(name="tpool", bufs=LR + 2))
        opool = ctx.enter_context(tc.tile_pool(name="opool", bufs=5))
        bpool = ctx.enter_context(tc.tile_pool(name="bpool", bufs=2))
        stat = ctx.enter_context(tc.tile_pool(name="stat", bufs=6))
        ps_t = ctx.enter_context(tc.psum_pool(name="ps_t", bufs=2))
        ps_m = ctx.enter_context(tc.psum_pool(name="ps_m", bufs=4))
        ps_g = ctx.enter_context(tc.psum_pool(name="ps_g", bufs=1))
        ctx.enter_context(tc.manual_schedule())

        ident = const.tile([P, P], F32, name="ident")
        ones = const.tile([P, P], BF16, name="ones")
        cst = const.tile([P, 2 * E], BF16, name="cst")
        b2_bc = const.tile([P, E], BF16, name="b2_bc")
        eps_t = const.tile([P, 1], F32, name="eps_t")
        warm = const.tile([P, 1], F32, name="warm")
        junk = const.tile([P, E], BF16, name="junk")
        w_codes = const.tile([P, E], U32, name="w_codes", align_bytes=64)
        w_scales = const.tile([P, E], U8, name="w_scales", align_bytes=64)
        w_raw = [const.tile([P, J, BANK], BF16, name="w_raw%d" % c) for c in range(2)]
        w_grp = [const.tile([P, J * BANK], BF16, name="w_grp%d" % c, align_bytes=64) for c in range(2)]
        h_first = [const.tile([P, E], BF16, name="h_first%d" % j) for j in range(J)]
        g2_ps = [ps_g.tile([P, BANK], F32, name="g2_ps%d" % c) for c in range(2)]

        y_sb, h_sb, xt, grp, codes, scales, o8 = {}, {}, {}, {}, {}, {}, {}
        hb, mm, r, rsum, negmu, ssq, std, rstd, t, o0t = {}, {}, {}, {}, {}, {}, {}, {}, {}, {}

        def rows(ap, g):
            return ap[g * GROUP : (g + 1) * GROUP, :]

        def load_y(g):
            y_sb[g] = ypool.tile([P, J, K], BF16, name="y_sb")
            nc.sync.dma_start(out=y_sb[g][:], in_=rows(yf, g).rearrange("(p j) k -> p j k", j=J))

        def load_h(g):
            h_sb[g] = hpool.tile([P, J, E], BF16, name="h_sb")
            nc.sync.dma_start(out=h_sb[g][:], in_=rows(hf, g).rearrange("(p j) n -> p j n", j=J))

        def load_h_first(j):
            nc.sync.dma_start(out=h_first[j][:], in_=rows(hf, 0).rearrange("(p j) n -> p j n", j=J)[:, j, :])

        def load_w(c):
            nc.sync.dma_start(
                out=w_raw[c][:], in_=W2[:, c * BANK : (c + 1) * BANK].rearrange("(p j) n -> p j n", j=J)
            )

        def transposes(g):
            xt[g] = []
            for b in range(2):
                bank = ps_t.tile([P, 2, 2, P], F32, name="xt")
                xt[g].append(bank)
                for a in range(2):
                    words = y_sb[g][:, 2 * b + a, :].bitcast(F32)
                    for u in range(2):
                        nc.tensor.transpose(bank[:, a, u, :], words[:, u : K // 2 : 2], ident[:])

        def empty_transposes(g, b):
            if b == 0:
                grp[g] = qpool.tile([P, 4 * GROUP], BF16, name="grp", align_bytes=64)
            dst = grp[g][:].bitcast(F32)[:, b * BANK : (b + 1) * BANK].rearrange("q (a t u) -> q a t u", a=2, u=2)
            src = xt[g][b][:].rearrange("q a u t -> q a t u")
            if emptier(g, b) == "V":
                nc.vector.tensor_copy(out=dst, in_=src)
            else:
                nc.scalar.copy(out=dst, in_=src)

        def quantize_y(g):
            codes[g] = qpool.tile([P, GROUP], U32, name="codes", align_bytes=64)
            scales[g] = qpool.tile([P, GROUP], U8, name="scales", align_bytes=64)
            nc.vector.quantize_mx(out=codes[g][:].bitcast(FP8X4), scales=scales[g][:], in_=grp[g][:])

        def interleave_w(c, half, engine):
            cols = slice(half * BANK // 2, (half + 1) * BANK // 2)
            dst = w_grp[c][:].rearrange("p (n j) -> p n j", j=J)[:, cols, :]
            src = w_raw[c][:, :, cols].rearrange("p j n -> p n j")
            if engine == "V":
                nc.vector.tensor_copy(out=dst, in_=src)
            else:
                nc.scalar.copy(out=dst, in_=src)

        def quantize_w(c):
            cols = slice(c * BANK, (c + 1) * BANK)
            nc.vector.quantize_mx(out=w_codes[:, cols].bitcast(FP8X4), scales=w_scales[:, cols], in_=w_grp[c][:])

        def add_bias(i):
            g, j = divmod(i, J)
            hb[i] = hbpool.tile([P, E], F32, name="hb")
            src = h_first[j][:] if g == 0 else h_sb[g][:, j, :]
            if i == 0:
                for c in range(2):
                    cols = slice(c * BANK, (c + 1) * BANK)
                    nc.vector.tensor_tensor(out=hb[i][:, cols], in0=src[:, cols], in1=b2_ps[c][:], op=ALU.add)
            else:
                nc.gpsimd.tensor_tensor(out=hb[i][:], in0=src, in1=b2_bc[:], op=ALU.add)

        def matmuls(i):
            g, j = divmod(i, J)
            toks = slice(j * P, (j + 1) * P)
            mm[i] = []
            for c in range(2):
                cols = slice(c * BANK, (c + 1) * BANK)
                acc = ps_m.tile([P, BANK], F32, name="acc")
                mm[i].append(acc)
                nc.tensor.matmul_mx(
                    out=acc[:],
                    lhsT=codes[g][:, toks].bitcast(FP8X4),
                    lhsT_scale=scales[g][:, toks],
                    rhs=w_codes[:, cols].bitcast(FP8X4),
                    rhs_scale=w_scales[:, cols],
                    start=True,
                    stop=True,
                )

        def residual(i):
            r[i] = rpool.tile([P, E], F32, name="r")
            rsum[i] = stat.tile([P, 2], F32, name="rsum")
            for c in range(2):
                cols = slice(c * BANK, (c + 1) * BANK)
                nc.vector.scalar_tensor_tensor(
                    out=r[i][:, cols],
                    in0=mm[i][c][:],
                    scalar=1.0,
                    in1=hb[i][:, cols],
                    op0=ALU.mult,
                    op1=ALU.add,
                    accum_out=rsum[i][:, c : c + 1],
                )

        def mean(i):
            negmu[i] = stat.tile([P, 1], F32, name="negmu")
            part = stat.tile([P, 2], F32, name="part")
            nc.vector.tensor_scalar(
                out=part[:],
                in0=rsum[i][:],
                scalar1=-1.0 / E,
                scalar2=None,
                op0=ALU.mult,
                op1=ALU.add,
                accum_out=negmu[i][:],
            )

        def squares(i):
            ssq[i] = stat.tile([P, 1], F32, name="ssq")
            nc.scalar.activation(
                out=junk[:], in_=r[i][:], func=ACT.Square, bias=negmu[i][:, 0:1], scale=1.0, accum_out=ssq[i][:]
            )

        def root(i):
            std[i] = stat.tile([P, 1], F32, name="std")
            nc.scalar.activation(out=std[i][:], in_=ssq[i][:], func=ACT.Sqrt, bias=eps_t[:, 0:1], scale=1.0 / E)

        def recip(i):
            rstd[i] = stat.tile([P, 1], F32, name="rstd")
            nc.vector.reciprocal(out=rstd[i][:], in_=std[i][:])

        def gain(i):
            t[i] = tpool.tile([P, E], F32, name="t")
            for c in range(2):
                cols = slice(c * BANK, (c + 1) * BANK)
                nc.vector.scalar_tensor_tensor(
                    out=t[i][:, cols],
                    in0=r[i][:, cols],
                    scalar=negmu[i][:, 0:1],
                    in1=g2_ps[c][:],
                    op0=ALU.add,
                    op1=ALU.mult,
                )

        def scale_by_rstd(i):
            o0t[i] = opool.tile([P, E], F32, name="o0t")
            if scaler(i) == "S":
                nc.scalar.activation(out=o0t[i][:], in_=t[i][:], func=ACT.Copy, scale=rstd[i][:, 0:1])
            elif scaler(i) == "V":
                nc.vector.tensor_scalar(out=o0t[i][:], in0=t[i][:], scalar1=rstd[i][:, 0:1], scalar2=None, op0=ALU.mult)
            else:
                nc.gpsimd.tensor_scalar(
                    out=o0t[i][:], in0=t[i][:], scalar1=rstd[i][:, 0:1], scalar2=0.0, op0=ALU.mult, op1=ALU.add
                )

        def cast(i):
            g, j = divmod(i, J)
            if j == 0:
                o8[g] = bpool.tile([P, J * E], FP8, name="o8")
            nc.scalar.activation(
                out=o8[g][:, j * E : (j + 1) * E], in_=o0t[i][:], func=ACT.Copy, scale=Y_SCALE, saturate=False
            )

        def store_f32(i):
            g, j = divmod(i, J)
            nc.sync.dma_start(out=rows(o0f, g).rearrange("(p j) n -> p j n", j=J)[:, j, :], in_=o0t[i][:])

        def store_bytes(g):
            nc.sync.dma_start(out=rows(o1f, g).rearrange("(p j) n -> p (j n)", j=J), in_=o8[g][:].bitcast(U8))

        def store_bytes_of_tile(i):
            g, j = divmod(i, J)
            nc.sync.dma_start(
                out=rows(o1f, g).rearrange("(p j) n -> p j n", j=J)[:, j, :],
                in_=o8[g][:, j * E : (j + 1) * E].bitcast(U8),
            )

        nc.vector.memset(cst[:], 0.0)
        nc.vector.memset(ones[:], 1.0)
        nc.vector.memset(eps_t[:], EPS)
        make_identity(nc, ident[:])
        nc.scalar.dma_start(out=cst[0:1, 0:E], in_=b2.unsqueeze(0))
        nc.scalar.dma_start(out=cst[0:1, E : 2 * E], in_=g2.unsqueeze(0))
        load_w(0)
        load_h_first(0)
        load_y(0)
        load_w(1)
        for j in range(1, J):
            load_h_first(j)
        for g in range(1, 4):
            load_y(g)
            load_h(g)
        load_h(4)
        nc.scalar.activation(out=warm[:], in_=eps_t[:], func=ACT.Sqrt)

        b2_ps = []
        for c in range(2):
            acc = ps_m.tile([P, BANK], F32, name="acc")
            b2_ps.append(acc)
            nc.tensor.matmul(acc[:], lhsT=ones[:], rhs=cst[:, c * BANK : (c + 1) * BANK], start=True, stop=True)
        for c in range(2):
            nc.tensor.matmul(
                g2_ps[c][:], lhsT=ones[:], rhs=cst[:, E + c * BANK : E + (c + 1) * BANK], start=True, stop=True
            )
        interleave_w(0, 0, "V")
        interleave_w(0, 1, "S")
        add_bias(0)
        transposes(0)
        quantize_w(0)
        interleave_w(1, 0, "V")
        interleave_w(1, 1, "S")
        empty_transposes(0, 0)
        empty_transposes(0, 1)
        quantize_w(1)
        quantize_y(0)
        for c in range(2):
            nc.scalar.copy(out=b2_bc[:, c * BANK : (c + 1) * BANK], in_=b2_ps[c][:])
        matmuls(0)
        transposes(1)
        for i in range(1, LA):
            add_bias(i)

        for s in range(NT + LR + 1):
            g, j = divmod(s, J)
            si = s - LR
            fi = s - LR - 1
            if s + LA < NT:
                add_bias(s + LA)
            if s + 1 < NT:
                matmuls(s + 1)
            if j == 3 and g + 2 < NG:
                transposes(g + 2)
            if s < NT:
                residual(s)
            if s == NT - 1:
                mean(s)
            if 0 <= s - 1 < NT:
                gain(s - 1)
            if s < NT - 1:
                mean(s)
            if j == 2 and g + 1 < NG:
                quantize_y(g + 1)
            if 0 <= si < NT:
                recip(si)
            if g + 1 < NG and j in (0, 1):
                empty_transposes(g + 1, j)
            if 0 <= si < NT and scaler(si) == "V":
                scale_by_rstd(si)
            if s < NT:
                squares(s)
            if 0 <= fi < NT:
                cast(fi)
            if s < NT:
                root(s)
            if 0 <= si < NT and scaler(si) != "V":
                scale_by_rstd(si)
            if j == 1 and g + 4 < NG:
                load_y(g + 4)
                if g > 0:
                    load_h(g + 4)
            if 0 <= si < NT:
                store_f32(si)
            if 0 <= fi < NT:
                if fi >= NT - J:
                    store_bytes_of_tile(fi)
                elif fi % J == J - 1:
                    store_bytes(fi // J)
